import numpy as np
import ml_dtypes


def mxq(x, axis, fmt="e4m3"):
    dtype, down = {"e4m3": (ml_dtypes.float8_e4m3fn, 7), "e5m2": (ml_dtypes.float8_e5m2, 14)}[fmt]
    v = np.moveaxis(np.asarray(x, np.float32).astype(ml_dtypes.bfloat16).astype(np.float64), axis, -1)
    blocks = v.reshape(v.shape[:-1] + (-1, 32))
    amax = np.abs(blocks).max(-1, keepdims=True)
    byte = np.maximum(np.where(amax > 0, np.frexp(amax)[1] - 1 + 127, 0) - down, 1)
    scale = np.exp2(byte - 127.0)
    codes = (blocks / scale).astype(np.float32).astype(dtype).astype(np.float64)
    return np.moveaxis((codes * scale).reshape(v.shape), -1, axis)


WIDE = False


def mx_kscale(k):
    if not WIDE:
        return np.ones(k)
    levels = np.array([30, -30])
    if k % 512:
        return np.exp2(np.random.permutation(np.resize(levels, k // 32))).repeat(32)
    a = np.empty((k // 512, 16))
    for p in range(k // 512):
        a[p, :8] = np.random.permutation(np.resize(levels, 8))
        for g in range(8):
            far = levels[np.abs(levels - a[p, g]) >= 10]
            a[p, g + 8] = far[np.random.randint(len(far))]
    return np.exp2(a.ravel()).repeat(32)


BF16 = ml_dtypes.bfloat16


def bf(x):
    return np.asarray(x, np.float32).astype(BF16)


def f64(x):
    return np.asarray(x).astype(np.float64)


N, S, K, Yd, Xd = 1024, 4, 16, 1024, 512
LOG_2PI = np.log(2.0 * np.pi)


def softplus(v):
    return np.maximum(v, 0.0) + np.log(1.0 + np.exp(-np.abs(v)))


def log_softmax(v, axis):
    m = v - v.max(axis, keepdims=True)
    return m - np.log(np.exp(m).sum(axis, keepdims=True))


def mv_gaussian_log_prob(value, mu, sig_diags, event_shape):
    diff = value - mu
    M = np.sum((diff / sig_diags) ** 2, axis=-1)
    half_log_det = np.sum(np.log(sig_diags), axis=-1)
    return -0.5 * (event_shape * LOG_2PI + M) - half_log_det


def setup_inputs():
    s = mx_kscale(Yd)
    return {"Y": bf(np.random.standard_normal((N, Yd)) * 0.5 * s),
            "We_mu": bf(np.random.standard_normal((Yd, Xd)) * 2.0 / np.sqrt(Yd) / s[:, None]),
            "be_mu": bf(np.random.standard_normal(Xd) * 0.1),
            "We_sig": bf(np.random.standard_normal((Yd, Xd)) * 1.0 / np.sqrt(Yd) / s[:, None]),
            "be_sig": bf(-3.0 + np.random.standard_normal(Xd) * 0.1),
            "phi_mus": bf(np.random.standard_normal((K, Xd)) * 3.0 / np.sqrt(Xd)),
            "phi_sigs": bf(1.0 + (np.random.random_sample((K, Xd)) - 0.5) * 9.0 / np.sqrt(Xd)),
            "phi_logits": bf(np.random.standard_normal(K))}


def reference(Y, We_mu, be_mu, We_sig, be_sig, phi_mus, phi_sigs, phi_logits):
    Yq = mxq(f64(Y), 1, "e5m2")
    enc_mu = (Yq @ mxq(f64(We_mu), 0, "e5m2")) + f64(be_mu)
    enc_sig = softplus((Yq @ mxq(f64(We_sig), 0, "e5m2")) + f64(be_sig)) + 1e-3
    log_pi = log_softmax(f64(phi_logits), -1)
    std_k = enc_sig[:, None, :] + f64(phi_sigs)[None, :, :]
    z_logits = log_pi[None, :] + mv_gaussian_log_prob(enc_mu[:, None, :], f64(phi_mus)[None, :, :], std_k, Xd)
    z_log_probs = log_softmax(z_logits, -1)
    return enc_mu, enc_sig, z_log_probs

@@ -1,0 +1,388 @@
+import math
+from contextlib import ExitStack
+
+import concourse.mybir as mybir
+from concourse.masks import make_identity
+
+N, KC, YD, XD = 1024, 16, 1024, 512
+FLOPS = 2 * N * YD * XD * 2
+
+F32 = mybir.dt.float32
+BF16 = mybir.dt.bfloat16
+U32 = mybir.dt.uint32
+U8 = mybir.dt.uint8
+FP8X4 = mybir.dt.float8_e5m2_x4
+ACT = mybir.ActivationFunctionType
+ALU = mybir.AluOpType
+AX = mybir.AxisListType
+
+P = 128
+NT = N // P
+NJ = XD // P
+G = YD // 512
+CH = 512
+TPC = CH // P
+PERIODS = (N // CH) * KC
+ROW_MU, ROW_SIG, ROW_BMU, ROW_BSIG, ROW_LOGIT = 0, 16, 32, 33, 34
+SIG_RING = 24
+T_RING = 12
+LN_START = 22
+LN_LEN = 3
+VECTOR_FIXED = 8
+TABLE_SWITCH = 3
+L_PER_STEP = 3
+EPS_FACTOR = math.exp(1e-3)
+
+
+def tile_deepgmm_pa_kernel(tc, Y, We_mu, be_mu, We_sig, be_sig, phi_mus, phi_sigs, phi_logits,
+                                       out_0, out_1, out_2):
+    nc = tc.nc
+    y_rows = Y.rearrange("(p t) k -> p t k", t=NT)
+    mu_rows = out_0.rearrange("(p t) d -> p t d", t=NT)
+    sig_rows = out_1.rearrange("(p t) d -> p t d", t=NT)
+    z_rows = out_2.rearrange("(p t) k -> p t k", t=NT)
+
+    with ExitStack() as ctx:
+        keep = ctx.enter_context(tc.tile_pool(name="keep", bufs=1))
+        psum = ctx.enter_context(tc.psum_pool(name="psum", bufs=1))
+        ctx.enter_context(tc.manual_schedule())
+
+        def bank(b, shape, dtype=F32):
+            return psum.tile(shape, dtype, name="bank%d" % b)
+
+        params = keep.tile([P, XD], BF16)
+        ident16 = keep.tile([P, P], BF16)
+        ident32 = keep.tile([P, P], F32)
+        ones = keep.tile([P, 1], F32)
+        par_t = keep.tile([P, NJ, ROW_BMU + 1], F32)
+        centre = keep.tile([P, NJ, KC], F32)
+        inv_p = keep.tile([P, NJ, KC], F32)
+        inv_p2 = keep.tile([P, NJ, KC], F32)
+        ln_p = keep.tile([P, NJ, KC], F32)
+        bias_mu = keep.tile([P, XD], F32)
+        bias_sig = keep.tile([P, XD], F32)
+        logit = keep.tile([P, KC], F32)
+        z_const = keep.tile([P, KC], F32)
+        y_codes = keep.tile([P, G, N], U32, align_bytes=64)
+        y_scales = keep.tile([P, G, N], U8, align_bytes=64)
+        w_codes = keep.tile([P, 2, G, XD], U32, align_bytes=64)
+        w_scales = keep.tile([P, 2, G, XD], U8, align_bytes=64)
+        soft = keep.tile([P, NT, XD], F32)
+        mu_out = keep.tile([P, 4, XD], F32)
+        ln_s = keep.tile([P, NJ, N], F32)
+        t_ring = keep.tile([P, T_RING, CH], F32)
+        pair = keep.tile([P, 4, CH], F32)
+        z_sq = keep.tile([P, NT, KC], F32)
+
+        SIG, MU = 0, 1
+
+        def mx(out, lhs_codes, lhs_scales, rhs_codes, rhs_scales):
+            for g in range(G):
+                nc.tensor.matmul_mx(out=out, lhsT=lhs_codes(g).bitcast(FP8X4), lhsT_scale=lhs_scales(g),
+                                    rhs=rhs_codes(g).bitcast(FP8X4), rhs_scale=rhs_scales(g),
+                                    start=(g == 0), stop=(g == G - 1))
+
+        def encode_rows(b, which, t):
+            acc = bank(b, [P, XD])
+            rows = slice(t * P, (t + 1) * P)
+            mx(acc[:], lambda g: y_codes[:, g, rows], lambda g: y_scales[:, g, rows],
+               lambda g: w_codes[:, which, g, :], lambda g: w_scales[:, which, g, :])
+            return acc
+
+        mu_t = {}
+
+        def encode_mu_t(c, j):
+            acc = bank(j, [P, CH])
+            cols = slice(j * P, (j + 1) * P)
+            rows = slice(c * CH, (c + 1) * CH)
+            mx(acc[:], lambda g: w_codes[:, MU, g, cols], lambda g: w_scales[:, MU, g, cols],
+               lambda g: y_codes[:, g, rows], lambda g: y_scales[:, g, rows])
+            mu_t[c, j] = acc
+
+        with tc.tile_pool(name="head", bufs=1) as head:
+            w_raw = head.tile([P, 2, G, 4, XD], BF16)
+            w_grp = head.tile([P, 2, XD, 4], BF16, align_bytes=64)
+            y_raw = head.tile([P, NT, YD], BF16)
+            y_grp = head.tile([P, 4, 2 * P * 4], BF16, align_bytes=64)
+            pre = head.tile([P, NT, XD], F32)
+
+            nc.vector.memset(params[:], 0.0)
+            nc.vector.memset(ones[:], 1.0)
+            make_identity(nc, ident16[:])
+            make_identity(nc, ident32[:])
+
+            def load_w(which, src, g):
+                nc.sync.dma_start(out=w_raw[:, which, g],
+                                  in_=src[g * 512:(g + 1) * 512, :].rearrange("(p j) c -> p j c", j=4))
+
+            def load_y(h):
+                nc.sync.dma_start(out=y_raw[:, 2 * h:2 * h + 2, :], in_=y_rows[:, 2 * h:2 * h + 2, :])
+
+            load_w(SIG, We_sig, 0)
+            load_y(0)
+            load_w(SIG, We_sig, 1)
+            for h in range(1, 4):
+                load_y(h)
+            load_w(MU, We_mu, 0)
+            load_w(MU, We_mu, 1)
+            nc.scalar.dma_start(out=params[ROW_MU:ROW_MU + KC, :], in_=phi_mus)
+            nc.scalar.dma_start(out=params[ROW_SIG:ROW_SIG + KC, :], in_=phi_sigs)
+            nc.scalar.dma_start(out=params[ROW_BMU:ROW_BMU + 1, :], in_=be_mu.unsqueeze(0))
+            nc.scalar.dma_start(out=params[ROW_BSIG:ROW_BSIG + 1, :], in_=be_sig.unsqueeze(0))
+            nc.scalar.dma_start(out=params[ROW_LOGIT:ROW_LOGIT + 1, 0:KC], in_=phi_logits.unsqueeze(0))
+
+            def spread_row(out, row, width):
+                nc.tensor.matmul(out, lhsT=ident16[:, row:row + 1].to_broadcast([P, P]), rhs=params[:, 0:width],
+                                 start=True, stop=True)
+
+            par_ps = bank(7, [P, NJ, P], BF16)
+            for j in range(NJ):
+                nc.tensor.transpose(par_ps[:, j, :], params[:, j * P:(j + 1) * P], ident16[:])
+            nc.scalar.copy(out=par_t[:], in_=par_ps[:, :, 0:ROW_BMU + 1])
+            bs_ps = bank(6, [P, XD])
+            spread_row(bs_ps[:], ROW_BSIG, XD)
+            nc.scalar.copy(out=bias_sig[:], in_=bs_ps[:])
+            bm_ps = bank(5, [P, XD])
+            spread_row(bm_ps[:], ROW_BMU, XD)
+            nc.scalar.copy(out=bias_mu[:], in_=bm_ps[:])
+
+            def interleave_w(which, g):
+                nc.vector.tensor_copy(out=w_grp[:, g].rearrange("p (c i) t -> p c t i", i=4),
+                                      in_=w_raw[:, which, g].rearrange("p t (c i) -> p c t i", i=4))
+
+            def quantize_w(which, g):
+                nc.vector.quantize_mx(out=w_codes[:, which, g, :].bitcast(FP8X4), scales=w_scales[:, which, g, :],
+                                      in_=w_grp[:, g].rearrange("p c t -> p (c t)"))
+
+            y_words = y_raw[:].bitcast(F32)
+
+            def turn_y(h):
+                for g in range(G):
+                    slot = (G * h + g) % 4
+                    xt = bank(slot, [P, 2, 2, P])
+                    for q in range(2):
+                        for u in range(2):
+                            nc.tensor.transpose(xt[:, q, u, :],
+                                                y_words[:, 2 * h + q, 256 * g + u:256 * (g + 1):2], ident32[:])
+                    nc.scalar.copy(out=y_grp[:, slot, :].bitcast(F32).rearrange("p (q r u) -> p q r u", q=2, u=2),
+                                   in_=xt[:].rearrange("p q u r -> p q r u"))
+
+            def quantize_y(h, g):
+                rows = slice(2 * h * P, 2 * (h + 1) * P)
+                nc.vector.quantize_mx(out=y_codes[:, g, rows].bitcast(FP8X4), scales=y_scales[:, g, rows],
+                                      in_=y_grp[:, (G * h + g) % 4, :])
+
+            def pre_act(t):
+                acc = encode_rows(4 + t % 3, SIG, t)
+                nc.vector.tensor_tensor(out=pre[:, t, :], in0=acc[:], in1=bias_sig[:], op=ALU.add)
+
+            def exp_neg_abs(h):
+                two = slice(2 * h, 2 * h + 2)
+                nc.vector.scalar_tensor_tensor(out=soft[:, two, :], in0=pre[:, two, :], scalar=-1.0,
+                                               in1=pre[:, two, :], op0=ALU.mult, op1=ALU.min)
+                nc.scalar.activation(out=soft[:, two, :], in_=soft[:, two, :], func=ACT.Exp)
+
+            interleave_w(SIG, 0)
+            turn_y(0)
+            phi_sig_t = par_t[:, :, ROW_SIG:ROW_SIG + KC]
+            nc.vector.reciprocal(out=inv_p[:], in_=phi_sig_t)
+            quantize_w(SIG, 0)
+            interleave_w(SIG, 1)
+            nc.vector.tensor_tensor(out=centre[:], in0=par_t[:, :, ROW_MU:ROW_MU + KC],
+                                    in1=par_t[:, :, ROW_BMU:ROW_BMU + 1].to_broadcast([P, NJ, KC]), op=ALU.subtract)
+            nc.vector.tensor_tensor(out=inv_p2[:], in0=inv_p[:], in1=inv_p[:], op=ALU.mult)
+            turn_y(1)
+            quantize_y(0, 0)
+            quantize_w(SIG, 1)
+            quantize_y(0, 1)
+            for h in range(4):
+                if h + 1 < 4:
+                    quantize_y(h + 1, 0)
+                    quantize_y(h + 1, 1)
+                pre_act(2 * h)
+                pre_act(2 * h + 1)
+                if h + 2 < 4:
+                    turn_y(h + 2)
+                if h >= 2:
+                    interleave_w(MU, h - 2)
+                exp_neg_abs(h)
+            quantize_w(MU, 0)
+            quantize_w(MU, 1)
+
+            nc.scalar.activation(out=ln_p[:], in_=phi_sig_t, func=ACT.Ln)
+            for h in range(4):
+                two = slice(2 * h, 2 * h + 2)
+                nc.scalar.activation(out=soft[:, two, :], in_=soft[:, two, :], func=ACT.Ln,
+                                     scale=EPS_FACTOR, bias=EPS_FACTOR)
+                nc.vector.scalar_tensor_tensor(out=soft[:, two, :], in0=pre[:, two, :], scalar=0.0,
+                                               in1=soft[:, two, :], op0=ALU.max, op1=ALU.add)
+                nc.sync.dma_start(out=sig_rows[:, two, :], in_=soft[:, two, :])
+
+        for j in range(NJ):
+            encode_mu_t(0, j)
+        const_ps = bank(7, [P, 2, KC])
+        spread_row(const_ps[:, 0, :], ROW_LOGIT, KC)
+        for j in range(NJ):
+            nc.tensor.matmul(const_ps[:, 1, :], lhsT=ones[:].to_broadcast([P, P]), rhs=ln_p[:, j, :],
+                             start=(j == 0), stop=(j == NJ - 1))
+        nc.vector.tensor_copy(out=logit[:], in_=const_ps[:, 0, :])
+        use = 8
+        for c in range(N // CH):
+            for j in range(NJ):
+                st = bank(4 + use % 3, [P, TPC, P])
+                use += 1
+                for q in range(TPC):
+                    nc.tensor.transpose(st[:, q, :], soft[:, c * TPC + q, j * P:(j + 1) * P], ident32[:])
+                nc.scalar.activation(out=ln_s[:, j, c * CH:(c + 1) * CH], in_=st[:].rearrange("p q r -> p (q r)"),
+                                     func=ACT.Ln)
+        for t in range(NT):
+            acc = encode_rows(4 + use % 3, MU, t)
+            use += 1
+            nc.vector.tensor_tensor(out=mu_out[:, t % 4, :], in0=acc[:], in1=bias_mu[:], op=ALU.add)
+            if t == 0:
+                nc.vector.tensor_tensor(out=z_const[:], in0=logit[:], in1=const_ps[:, 1, :], op=ALU.subtract)
+            if t % 2 == 1:
+                nc.sync.dma_start(out=mu_rows[:, t - 1:t + 1, :], in_=mu_out[:, t % 4 - 1:t % 4 + 1, :])
+
+        main = ctx.enter_context(tc.tile_pool(name="main", bufs=1))
+        ratio = main.tile([P, SIG_RING, CH], F32)
+        prod = main.tile([P, PERIODS, CH], F32)
+        z_ln = bank(7, [P, NT, KC])
+
+        def sigmoid(x):
+            i, j = divmod(x, NJ)
+            c, k = divmod(i, KC)
+            nc.scalar.activation(out=ratio[:, x % SIG_RING, :], in_=ln_s[:, j, c * CH:(c + 1) * CH],
+                                 func=ACT.Sigmoid, scale=-1.0, bias=ln_p[:, j, k:k + 1])
+
+        def r_of(i, j):
+            return ratio[:, (NJ * i + j) % SIG_RING, :]
+
+        def t_of(i, j):
+            return t_ring[:, (NJ * i + j) % T_RING, :]
+
+        def whiten(i, j):
+            c, k = divmod(i, KC)
+            nc.vector.scalar_tensor_tensor(out=t_of(i, j), in0=mu_t[c, j][:], scalar=centre[:, j, k:k + 1],
+                                           in1=r_of(i, j), op0=ALU.subtract, op1=ALU.mult)
+
+        def square_scalar(i, j):
+            k = i % KC
+            nc.scalar.activation(out=t_of(i, j), in_=t_of(i, j), func=ACT.Square, scale=inv_p[:, j, k:k + 1])
+
+        def square_vector(i, j):
+            k = i % KC
+            nc.vector.scalar_tensor_tensor(out=t_of(i, j), in0=t_of(i, j), scalar=inv_p2[:, j, k:k + 1],
+                                           in1=t_of(i, j), op0=ALU.mult, op1=ALU.mult)
+
+        def pair_product(eng, i, half):
+            eng.tensor_tensor(out=pair[:, (2 * i + half) % 4, :], in0=r_of(i, 2 * half),
+                              in1=r_of(i, 2 * half + 1), op=ALU.mult)
+
+        def full_product(i):
+            nc.vector.tensor_tensor(out=prod[:, i, :], in0=pair[:, (2 * i) % 4, :],
+                                    in1=pair[:, (2 * i + 1) % 4, :], op=ALU.mult)
+
+        acc_of = {}
+
+        def turn_squares(i):
+            acc = bank(4 + (use + i) % 3, [P, TPC, P])
+            for q in range(TPC):
+                for j in range(NJ):
+                    nc.tensor.matmul(acc[:, q, :], lhsT=t_of(i, j)[:, q * P:(q + 1) * P], rhs=ident32[:],
+                                     is_transpose=True, start=(j == 0), stop=(j == NJ - 1))
+            acc_of[i] = acc
+
+        def reduce_squares(i):
+            c, k = divmod(i, KC)
+            nc.vector.tensor_reduce(out=z_sq[:, c * TPC:(c + 1) * TPC, k], in_=acc_of[i][:], axis=AX.X, op=ALU.add)
+
+        def log_product(i):
+            nc.scalar.activation(out=prod[:, i, :], in_=prod[:, i, :], func=ACT.Ln)
+
+        def sum_logs(i):
+            c, k = divmod(i, KC)
+            for q in range(TPC):
+                nc.tensor.matmul(z_ln[:, c * TPC + q, k:k + 1], lhsT=prod[:, i, q * P:(q + 1) * P], rhs=ones[:],
+                                 start=True, stop=True)
+
+        phases = [(0, LN_START), (LN_START + LN_LEN, PERIODS - LN_LEN)]
+        switches = (LN_START, LN_START + LN_LEN, PERIODS - LN_LEN)
+        sig_next, ln_next, sum_next, sq_credit = 0, 0, 0, 0.0
+        for x in range(NJ):
+            sigmoid(x)
+        sig_next = NJ
+        for i in range(PERIODS + 2):
+            sig_goal = sig_next
+            in_ln = True
+            for lo, hi in phases:
+                if lo <= i < hi:
+                    in_ln = False
+                    made = -(-NJ * (hi - lo + LN_LEN) * (i - lo + 1) // (hi - lo))
+                    sig_goal = min(NJ * (lo + 1) + made, NJ * PERIODS)
+            first = list(range(sig_next, sig_goal))
+            sig_next = sig_goal
+            logs = []
+            if in_ln:
+                end = LN_START + LN_LEN if i < LN_START + LN_LEN else PERIODS + 1
+                ready = min(i, PERIODS)
+                left = max(end - i, 1)
+                want = -(-(min(end - 1, PERIODS) - ln_next) // left)
+                logs = list(range(ln_next, min(ln_next + want, ready)))
+            sum_goal = min(ln_next, sum_next + L_PER_STEP)
+            ln_next += len(logs)
+            on_scalar = 0
+            if 1 <= i <= PERIODS:
+                table_work = len(first) + len(logs) + (TABLE_SWITCH if i in switches else 0)
+                sq_credit += min(max((VECTOR_FIXED + NJ - table_work) / 2, 0), NJ)
+                on_scalar = min(int(sq_credit), NJ)
+                sq_credit -= on_scalar
+
+            work = [(sigmoid, x) for x in first] + [(log_product, x) for x in logs]
+            for s in range(max(len(work), on_scalar)):
+                if s < len(work):
+                    work[s][0](work[s][1])
+                if s < on_scalar:
+                    square_scalar(i - 1, s)
+
+            live = i < PERIODS
+            if live:
+                whiten(i, 0)
+                pair_product(nc.vector, i, 0)
+                whiten(i, 1)
+                pair_product(nc.vector, i, 1)
+                whiten(i, 2)
+            if 1 <= i <= PERIODS:
+                for j in range(on_scalar, NJ):
+                    square_vector(i - 1, j)
+            if live:
+                whiten(i, 3)
+                full_product(i)
+            if i >= 2:
+                reduce_squares(i - 2)
+            if i == KC - 1:
+                for j in range(NJ):
+                    encode_mu_t(1, j)
+            for x in range(sum_next, sum_goal):
+                sum_logs(x)
+            sum_next = sum_goal
+            if 1 <= i <= PERIODS:
+                turn_squares(i - 1)
+        for x in range(sum_next, PERIODS):
+            sum_logs(x)
+
+        z = keep.tile([P, NT, KC], F32)
+        top = keep.tile([P, NT], F32)
+        e = keep.tile([P, NT, KC], F32)
+        total = keep.tile([P, NT], F32)
+        nc.vector.scalar_tensor_tensor(out=z[:], in0=z_sq[:], scalar=-0.5, in1=z_ln[:], op0=ALU.mult, op1=ALU.add)
+        nc.vector.tensor_tensor(out=z[:], in0=z[:], in1=z_const[:].unsqueeze(1).to_broadcast([P, NT, KC]), op=ALU.add)
+        nc.vector.tensor_reduce(out=top[:], in_=z[:], axis=AX.X, op=ALU.max)
+        nc.vector.tensor_tensor(out=z[:], in0=z[:], in1=top[:].unsqueeze(2).to_broadcast([P, NT, KC]),
+                                op=ALU.subtract)
+        nc.scalar.activation(out=e[:], in_=z[:], func=ACT.Exp)
+        nc.vector.tensor_reduce(out=total[:], in_=e[:], axis=AX.X, op=ALU.add)
+        nc.scalar.activation(out=total[:], in_=total[:], func=ACT.Ln)
+        nc.vector.tensor_tensor(out=e[:], in0=z[:], in1=total[:].unsqueeze(2).to_broadcast([P, NT, KC]),
+                                op=ALU.subtract)
+        nc.sync.dma_start(out=z_rows, in_=e[:])

@@ -26,11 +26,11 @@ PERIODS = (N // CH) * KC
 ROW_MU, ROW_SIG, ROW_BMU, ROW_BSIG, ROW_LOGIT = 0, 16, 32, 33, 34
 SIG_RING = 24
 T_RING = 12
-LN_START = 22
+LN_START = 14
 LN_LEN = 3
 VECTOR_FIXED = 8
 TABLE_SWITCH = 3
-L_PER_STEP = 3
+LOG_COST = 1.5
 EPS_FACTOR = math.exp(1e-3)
 
 
@@ -247,7 +247,8 @@ def tile_deepgmm_pa_kernel(tc, Y, We_mu, be_mu, We_sig, be_sig, phi_mus, phi_sig
         main = ctx.enter_context(tc.tile_pool(name="main", bufs=1))
         ratio = main.tile([P, SIG_RING, CH], F32)
         prod = main.tile([P, PERIODS, CH], F32)
-        z_ln = bank(7, [P, NT, KC])
+        z_ln = main.tile([P, NT, KC], F32)
+        ln_terms = main.tile([P, TPC, P], F32)
 
         def sigmoid(x):
             i, j = divmod(x, NJ)
@@ -286,7 +287,7 @@ def tile_deepgmm_pa_kernel(tc, Y, We_mu, be_mu, We_sig, be_sig, phi_mus, phi_sig
         acc_of = {}
 
         def turn_squares(i):
-            acc = bank(4 + (use + i) % 3, [P, TPC, P])
+            acc = bank(4 + i % 2, [P, TPC, P])
             for q in range(TPC):
                 for j in range(NJ):
                     nc.tensor.matmul(acc[:, q, :], lhsT=t_of(i, j)[:, q * P:(q + 1) * P], rhs=ident32[:],
@@ -297,51 +298,58 @@ def tile_deepgmm_pa_kernel(tc, Y, We_mu, be_mu, We_sig, be_sig, phi_mus, phi_sig
             c, k = divmod(i, KC)
             nc.vector.tensor_reduce(out=z_sq[:, c * TPC:(c + 1) * TPC, k], in_=acc_of[i][:], axis=AX.X, op=ALU.add)
 
-        def log_product(i):
-            nc.scalar.activation(out=prod[:, i, :], in_=prod[:, i, :], func=ACT.Ln)
+        turned = {}
 
-        def sum_logs(i):
+        def turn_product(i):
+            pt = bank(6 + i % 2, [P, TPC, P])
+            for q in range(TPC):
+                nc.tensor.transpose(pt[:, q, :], prod[:, i, q * P:(q + 1) * P], ident32[:])
+            turned[i] = pt
+
+        def log_product(i):
             c, k = divmod(i, KC)
             for q in range(TPC):
-                nc.tensor.matmul(z_ln[:, c * TPC + q, k:k + 1], lhsT=prod[:, i, q * P:(q + 1) * P], rhs=ones[:],
-                                 start=True, stop=True)
+                nc.scalar.activation(out=ln_terms[:, q, :], in_=turned[i][:, q, :], func=ACT.Ln,
+                                     accum_out=z_ln[:, c * TPC + q, k:k + 1])
 
         phases = [(0, LN_START), (LN_START + LN_LEN, PERIODS - LN_LEN)]
         switches = (LN_START, LN_START + LN_LEN, PERIODS - LN_LEN)
-        sig_next, ln_next, sum_next, sq_credit = 0, 0, 0, 0.0
+        sigs_of, logs_of = [], []
+        sig_next, ln_next = NJ, 0
+        for i in range(PERIODS + 3):
+            sig_goal, ln_goal = sig_next, ln_next
+            phase = [(lo, hi) for lo, hi in phases if lo <= i < hi]
+            if phase:
+                lo, hi = phase[0]
+                made = -(-NJ * (hi - lo + LN_LEN) * (i - lo + 1) // (hi - lo))
+                sig_goal = min(NJ * (lo + 1) + made, NJ * PERIODS)
+            else:
+                end = LN_START + LN_LEN if i < LN_START + LN_LEN else PERIODS + 1
+                want = -(-(end - 1 - ln_next) // max(end - i, 1))
+                ln_goal = min(ln_next + want, i, PERIODS)
+            sigs_of.append(list(range(sig_next, sig_goal)))
+            logs_of.append(list(range(ln_next, ln_goal)))
+            sig_next, ln_next = sig_goal, ln_goal
+
         for x in range(NJ):
             sigmoid(x)
-        sig_next = NJ
+        sq_credit = 0.0
         for i in range(PERIODS + 2):
-            sig_goal = sig_next
-            in_ln = True
-            for lo, hi in phases:
-                if lo <= i < hi:
-                    in_ln = False
-                    made = -(-NJ * (hi - lo + LN_LEN) * (i - lo + 1) // (hi - lo))
-                    sig_goal = min(NJ * (lo + 1) + made, NJ * PERIODS)
-            first = list(range(sig_next, sig_goal))
-            sig_next = sig_goal
-            logs = []
-            if in_ln:
-                end = LN_START + LN_LEN if i < LN_START + LN_LEN else PERIODS + 1
-                ready = min(i, PERIODS)
-                left = max(end - i, 1)
-                want = -(-(min(end - 1, PERIODS) - ln_next) // left)
-                logs = list(range(ln_next, min(ln_next + want, ready)))
-            sum_goal = min(ln_next, sum_next + L_PER_STEP)
-            ln_next += len(logs)
+            sigs, logs = sigs_of[i], logs_of[i]
             on_scalar = 0
             if 1 <= i <= PERIODS:
-                table_work = len(first) + len(logs) + (TABLE_SWITCH if i in switches else 0)
+                table_work = len(sigs) + LOG_COST * len(logs) + (TABLE_SWITCH if i in switches else 0)
                 sq_credit += min(max((VECTOR_FIXED + NJ - table_work) / 2, 0), NJ)
                 on_scalar = min(int(sq_credit), NJ)
                 sq_credit -= on_scalar
 
-            work = [(sigmoid, x) for x in first] + [(log_product, x) for x in logs]
-            for s in range(max(len(work), on_scalar)):
-                if s < len(work):
-                    work[s][0](work[s][1])
+            for s in range(max(len(sigs), len(logs), on_scalar)):
+                if s < len(sigs):
+                    sigmoid(sigs[s])
+                if s < len(logs):
+                    log_product(logs[s])
+                    if s + 2 < len(logs):
+                        turn_product(logs[s + 2])
                 if s < on_scalar:
                     square_scalar(i - 1, s)
 
@@ -363,13 +371,10 @@ def tile_deepgmm_pa_kernel(tc, Y, We_mu, be_mu, We_sig, be_sig, phi_mus, phi_sig
             if i == KC - 1:
                 for j in range(NJ):
                     encode_mu_t(1, j)
-            for x in range(sum_next, sum_goal):
-                sum_logs(x)
-            sum_next = sum_goal
+            for x in logs_of[i + 1][:2]:
+                turn_product(x)
             if 1 <= i <= PERIODS:
                 turn_squares(i - 1)
-        for x in range(sum_next, PERIODS):
-            sum_logs(x)
 
         z = keep.tile([P, NT, KC], F32)
         top = keep.tile([P, NT], F32)

@@ -28,7 +28,7 @@ SIG_RING = 24
 T_RING = 12
 LN_START = 14
 LN_LEN = 3
-VECTOR_FIXED = 8
+VECTOR_FIXED = 6
 TABLE_SWITCH = 3
 LOG_COST = 1.5
 EPS_FACTOR = math.exp(1e-3)
@@ -71,7 +71,7 @@ def tile_deepgmm_pa_kernel(tc, Y, We_mu, be_mu, We_sig, be_sig, phi_mus, phi_sig
         mu_out = keep.tile([P, 4, XD], F32)
         ln_s = keep.tile([P, NJ, N], F32)
         t_ring = keep.tile([P, T_RING, CH], F32)
-        pair = keep.tile([P, 4, CH], F32)
+        pair = keep.tile([P, 2, CH], F32)
         z_sq = keep.tile([P, NT, KC], F32)
 
         SIG, MU = 0, 1
@@ -135,17 +135,6 @@ def tile_deepgmm_pa_kernel(tc, Y, We_mu, be_mu, We_sig, be_sig, phi_mus, phi_sig
                 nc.tensor.matmul(out, lhsT=ident16[:, row:row + 1].to_broadcast([P, P]), rhs=params[:, 0:width],
                                  start=True, stop=True)
 
-            par_ps = bank(7, [P, NJ, P], BF16)
-            for j in range(NJ):
-                nc.tensor.transpose(par_ps[:, j, :], params[:, j * P:(j + 1) * P], ident16[:])
-            nc.scalar.copy(out=par_t[:], in_=par_ps[:, :, 0:ROW_BMU + 1])
-            bs_ps = bank(6, [P, XD])
-            spread_row(bs_ps[:], ROW_BSIG, XD)
-            nc.scalar.copy(out=bias_sig[:], in_=bs_ps[:])
-            bm_ps = bank(5, [P, XD])
-            spread_row(bm_ps[:], ROW_BMU, XD)
-            nc.scalar.copy(out=bias_mu[:], in_=bm_ps[:])
-
             def interleave_w(which, g):
                 nc.vector.tensor_copy(out=w_grp[:, g].rearrange("p (c i) t -> p c t i", i=4),
                                       in_=w_raw[:, which, g].rearrange("p t (c i) -> p c t i", i=4))
@@ -184,6 +173,17 @@ def tile_deepgmm_pa_kernel(tc, Y, We_mu, be_mu, We_sig, be_sig, phi_mus, phi_sig
 
             interleave_w(SIG, 0)
             turn_y(0)
+            par_ps = bank(7, [P, NJ, P], BF16)
+            for j in range(NJ):
+                nc.tensor.transpose(par_ps[:, j, :], params[:, j * P:(j + 1) * P], ident16[:])
+            nc.scalar.copy(out=par_t[:], in_=par_ps[:, :, 0:ROW_BMU + 1])
+            bs_ps = bank(6, [P, XD])
+            spread_row(bs_ps[:], ROW_BSIG, XD)
+            nc.scalar.copy(out=bias_sig[:], in_=bs_ps[:])
+            bm_ps = bank(5, [P, XD])
+            spread_row(bm_ps[:], ROW_BMU, XD)
+            nc.scalar.copy(out=bias_mu[:], in_=bm_ps[:])
+
             phi_sig_t = par_t[:, :, ROW_SIG:ROW_SIG + KC]
             nc.vector.reciprocal(out=inv_p[:], in_=phi_sig_t)
             quantize_w(SIG, 0)
@@ -276,13 +276,13 @@ def tile_deepgmm_pa_kernel(tc, Y, We_mu, be_mu, We_sig, be_sig, phi_mus, phi_sig
             nc.vector.scalar_tensor_tensor(out=t_of(i, j), in0=t_of(i, j), scalar=inv_p2[:, j, k:k + 1],
                                            in1=t_of(i, j), op0=ALU.mult, op1=ALU.mult)
 
-        def pair_product(eng, i, half):
-            eng.tensor_tensor(out=pair[:, (2 * i + half) % 4, :], in0=r_of(i, 2 * half),
-                              in1=r_of(i, 2 * half + 1), op=ALU.mult)
+        def pair_products(i):
+            base = (NJ * i) % SIG_RING
+            nc.gpsimd.tensor_tensor(out=pair[:], in0=ratio[:, base:base + NJ:2, :],
+                                    in1=ratio[:, base + 1:base + NJ:2, :], op=ALU.mult)
 
         def full_product(i):
-            nc.vector.tensor_tensor(out=prod[:, i, :], in0=pair[:, (2 * i) % 4, :],
-                                    in1=pair[:, (2 * i + 1) % 4, :], op=ALU.mult)
+            nc.vector.tensor_tensor(out=prod[:, i, :], in0=pair[:, 0, :], in1=pair[:, 1, :], op=ALU.mult)
 
         acc_of = {}
 
@@ -324,9 +324,9 @@ def tile_deepgmm_pa_kernel(tc, Y, We_mu, be_mu, We_sig, be_sig, phi_mus, phi_sig
                 made = -(-NJ * (hi - lo + LN_LEN) * (i - lo + 1) // (hi - lo))
                 sig_goal = min(NJ * (lo + 1) + made, NJ * PERIODS)
             else:
-                end = LN_START + LN_LEN if i < LN_START + LN_LEN else PERIODS + 1
-                want = -(-(end - 1 - ln_next) // max(end - i, 1))
-                ln_goal = min(ln_next + want, i, PERIODS)
+                end = LN_START + LN_LEN if i < LN_START + LN_LEN else PERIODS + 2
+                want = -(-(end - 2 - ln_next) // max(end - i, 1))
+                ln_goal = min(ln_next + want, i - 1, PERIODS)
             sigs_of.append(list(range(sig_next, sig_goal)))
             logs_of.append(list(range(ln_next, ln_goal)))
             sig_next, ln_next = sig_goal, ln_goal
@@ -353,19 +353,14 @@ def tile_deepgmm_pa_kernel(tc, Y, We_mu, be_mu, We_sig, be_sig, phi_mus, phi_sig
                 if s < on_scalar:
                     square_scalar(i - 1, s)
 
-            live = i < PERIODS
-            if live:
-                whiten(i, 0)
-                pair_product(nc.vector, i, 0)
-                whiten(i, 1)
-                pair_product(nc.vector, i, 1)
-                whiten(i, 2)
             if 1 <= i <= PERIODS:
                 for j in range(on_scalar, NJ):
                     square_vector(i - 1, j)
-            if live:
-                whiten(i, 3)
-                full_product(i)
+                full_product(i - 1)
+            if i < PERIODS:
+                pair_products(i)
+                for j in range(NJ):
+                    whiten(i, j)
             if i >= 2:
                 reduce_squares(i - 2)
             if i == KC - 1:

@@ -24,13 +24,13 @@ CH = 512
 TPC = CH // P
 PERIODS = (N // CH) * KC
 ROW_MU, ROW_SIG, ROW_BMU, ROW_BSIG, ROW_LOGIT = 0, 16, 32, 33, 34
-SIG_RING = 24
+SIG_RING = NJ * (7 + 2)
 T_RING = 12
-LN_START = 14
-LN_LEN = 3
+LN_LEN = 7
 VECTOR_FIXED = 6
 TABLE_SWITCH = 3
 LOG_COST = 1.5
+LEAD = 2
 EPS_FACTOR = math.exp(1e-3)
 
 
@@ -248,6 +248,7 @@ def tile_deepgmm_pa_kernel(tc, Y, We_mu, be_mu, We_sig, be_sig, phi_mus, phi_sig
         ratio = main.tile([P, SIG_RING, CH], F32)
         prod = main.tile([P, PERIODS, CH], F32)
         z_ln = main.tile([P, NT, KC], F32)
+        z_lin = main.tile([P, NT, KC], F32)
         ln_terms = main.tile([P, TPC, P], F32)
 
         def sigmoid(x):
@@ -312,34 +313,31 @@ def tile_deepgmm_pa_kernel(tc, Y, We_mu, be_mu, We_sig, be_sig, phi_mus, phi_sig
                 nc.scalar.activation(out=ln_terms[:, q, :], in_=turned[i][:, q, :], func=ACT.Ln,
                                      accum_out=z_ln[:, c * TPC + q, k:k + 1])
 
-        phases = [(0, LN_START), (LN_START + LN_LEN, PERIODS - LN_LEN)]
-        switches = (LN_START, LN_START + LN_LEN, PERIODS - LN_LEN)
+        ln_start = PERIODS - LN_LEN
         sigs_of, logs_of = [], []
-        sig_next, ln_next = NJ, 0
+        sig_next, ln_next = LEAD * NJ, 0
         for i in range(PERIODS + 3):
             sig_goal, ln_goal = sig_next, ln_next
-            phase = [(lo, hi) for lo, hi in phases if lo <= i < hi]
-            if phase:
-                lo, hi = phase[0]
-                made = -(-NJ * (hi - lo + LN_LEN) * (i - lo + 1) // (hi - lo))
-                sig_goal = min(NJ * (lo + 1) + made, NJ * PERIODS)
+            if i < ln_start:
+                sig_goal = LEAD * NJ + -(-NJ * (PERIODS - LEAD) * (i + 1) // ln_start)
             else:
-                end = LN_START + LN_LEN if i < LN_START + LN_LEN else PERIODS + 2
-                want = -(-(end - 2 - ln_next) // max(end - i, 1))
-                ln_goal = min(ln_next + want, i - 1, PERIODS)
+                want = -(-(PERIODS - ln_next) // max(PERIODS + 0 - i, 1))
+                ln_goal = min(ln_next + want, i, PERIODS)
             sigs_of.append(list(range(sig_next, sig_goal)))
             logs_of.append(list(range(ln_next, ln_goal)))
             sig_next, ln_next = sig_goal, ln_goal
 
-        for x in range(NJ):
+        for x in range(LEAD * NJ):
             sigmoid(x)
+            if x == NJ - 1:
+                pair_products(0)
         sq_credit = 0.0
         for i in range(PERIODS + 2):
             sigs, logs = sigs_of[i], logs_of[i]
             on_scalar = 0
             if 1 <= i <= PERIODS:
-                table_work = len(sigs) + LOG_COST * len(logs) + (TABLE_SWITCH if i in switches else 0)
-                sq_credit += min(max((VECTOR_FIXED + NJ - table_work) / 2, 0), NJ)
+                table_work = len(sigs) + LOG_COST * len(logs) + (TABLE_SWITCH if i == ln_start else 0)
+                sq_credit += min(max(((VECTOR_FIXED if i < PERIODS else 1) + NJ - table_work) / 2, 0), NJ)
                 on_scalar = min(int(sq_credit), NJ)
                 sq_credit -= on_scalar
 
@@ -356,11 +354,15 @@ def tile_deepgmm_pa_kernel(tc, Y, We_mu, be_mu, We_sig, be_sig, phi_mus, phi_sig
             if 1 <= i <= PERIODS:
                 for j in range(on_scalar, NJ):
                     square_vector(i - 1, j)
-                full_product(i - 1)
             if i < PERIODS:
-                pair_products(i)
+                full_product(i)
+                if i + 1 < PERIODS:
+                    pair_products(i + 1)
                 for j in range(NJ):
                     whiten(i, j)
+            if i == PERIODS + 1:
+                nc.vector.tensor_tensor(out=z_lin[:], in0=z_ln[:],
+                                        in1=z_const[:].unsqueeze(1).to_broadcast([P, NT, KC]), op=ALU.add)
             if i >= 2:
                 reduce_squares(i - 2)
             if i == KC - 1:
@@ -375,8 +377,7 @@ def tile_deepgmm_pa_kernel(tc, Y, We_mu, be_mu, We_sig, be_sig, phi_mus, phi_sig
         top = keep.tile([P, NT], F32)
         e = keep.tile([P, NT, KC], F32)
         total = keep.tile([P, NT], F32)
-        nc.vector.scalar_tensor_tensor(out=z[:], in0=z_sq[:], scalar=-0.5, in1=z_ln[:], op0=ALU.mult, op1=ALU.add)
-        nc.vector.tensor_tensor(out=z[:], in0=z[:], in1=z_const[:].unsqueeze(1).to_broadcast([P, NT, KC]), op=ALU.add)
+        nc.vector.scalar_tensor_tensor(out=z[:], in0=z_sq[:], scalar=-0.5, in1=z_lin[:], op0=ALU.mult, op1=ALU.add)
         nc.vector.tensor_reduce(out=top[:], in_=z[:], axis=AX.X, op=ALU.max)
         nc.vector.tensor_tensor(out=z[:], in0=z[:], in1=top[:].unsqueeze(2).to_broadcast([P, NT, KC]),
                                 op=ALU.subtract)

@@ -29,7 +29,7 @@ T_RING = 12
 LN_LEN = 7
 VECTOR_FIXED = 6
 TABLE_SWITCH = 3
-LOG_COST = 1.5
+LOG_COST = 1.9
 LEAD = 2
 EPS_FACTOR = math.exp(1e-3)
 

import math
from contextlib import ExitStack

import concourse.mybir as mybir
from concourse.masks import make_identity

N, KC, YD, XD = 1024, 16, 1024, 512
FLOPS = 2 * N * YD * XD * 2

F32 = mybir.dt.float32
BF16 = mybir.dt.bfloat16
U32 = mybir.dt.uint32
U8 = mybir.dt.uint8
FP8X4 = mybir.dt.float8_e5m2_x4
ACT = mybir.ActivationFunctionType
ALU = mybir.AluOpType
AX = mybir.AxisListType

P = 128
NT = N // P
NJ = XD // P
G = YD // 512
CH = 512
TPC = CH // P
PERIODS = (N // CH) * KC
ROW_MU, ROW_SIG, ROW_BMU, ROW_BSIG, ROW_LOGIT = 0, 16, 32, 33, 34
SIG_RING = NJ * (7 + 2)
T_RING = 12
LN_LEN = 7
VECTOR_FIXED = 6
TABLE_SWITCH = 3
LOG_COST = 1.9
LEAD = 2
EPS_FACTOR = math.exp(1e-3)


def tile_deepgmm_pa_kernel(tc, Y, We_mu, be_mu, We_sig, be_sig, phi_mus, phi_sigs, phi_logits,
                                       out_0, out_1, out_2):
    nc = tc.nc
    y_rows = Y.rearrange("(p t) k -> p t k", t=NT)
    mu_rows = out_0.rearrange("(p t) d -> p t d", t=NT)
    sig_rows = out_1.rearrange("(p t) d -> p t d", t=NT)
    z_rows = out_2.rearrange("(p t) k -> p t k", t=NT)

    with ExitStack() as ctx:
        keep = ctx.enter_context(tc.tile_pool(name="keep", bufs=1))
        psum = ctx.enter_context(tc.psum_pool(name="psum", bufs=1))
        ctx.enter_context(tc.manual_schedule())

        def bank(b, shape, dtype=F32):
            return psum.tile(shape, dtype, name="bank%d" % b)

        params = keep.tile([P, XD], BF16)
        ident16 = keep.tile([P, P], BF16)
        ident32 = keep.tile([P, P], F32)
        ones = keep.tile([P, 1], F32)
        par_t = keep.tile([P, NJ, ROW_BMU + 1], F32)
        centre = keep.tile([P, NJ, KC], F32)
        inv_p = keep.tile([P, NJ, KC], F32)
        inv_p2 = keep.tile([P, NJ, KC], F32)
        ln_p = keep.tile([P, NJ, KC], F32)
        bias_mu = keep.tile([P, XD], F32)
        bias_sig = keep.tile([P, XD], F32)
        logit = keep.tile([P, KC], F32)
        z_const = keep.tile([P, KC], F32)
        y_codes = keep.tile([P, G, N], U32, align_bytes=64)
        y_scales = keep.tile([P, G, N], U8, align_bytes=64)
        w_codes = keep.tile([P, 2, G, XD], U32, align_bytes=64)
        w_scales = keep.tile([P, 2, G, XD], U8, align_bytes=64)
        soft = keep.tile([P, NT, XD], F32)
        mu_out = keep.tile([P, 4, XD], F32)
        ln_s = keep.tile([P, NJ, N], F32)
        t_ring = keep.tile([P, T_RING, CH], F32)
        pair = keep.tile([P, 2, CH], F32)
        z_sq = keep.tile([P, NT, KC], F32)

        SIG, MU = 0, 1

        def mx(out, lhs_codes, lhs_scales, rhs_codes, rhs_scales):
            for g in range(G):
                nc.tensor.matmul_mx(out=out, lhsT=lhs_codes(g).bitcast(FP8X4), lhsT_scale=lhs_scales(g),
                                    rhs=rhs_codes(g).bitcast(FP8X4), rhs_scale=rhs_scales(g),
                                    start=(g == 0), stop=(g == G - 1))

        def encode_rows(b, which, t):
            acc = bank(b, [P, XD])
            rows = slice(t * P, (t + 1) * P)
            mx(acc[:], lambda g: y_codes[:, g, rows], lambda g: y_scales[:, g, rows],
               lambda g: w_codes[:, which, g, :], lambda g: w_scales[:, which, g, :])
            return acc

        mu_t = {}

        def encode_mu_t(c, j):
            acc = bank(j, [P, CH])
            cols = slice(j * P, (j + 1) * P)
            rows = slice(c * CH, (c + 1) * CH)
            mx(acc[:], lambda g: w_codes[:, MU, g, cols], lambda g: w_scales[:, MU, g, cols],
               lambda g: y_codes[:, g, rows], lambda g: y_scales[:, g, rows])
            mu_t[c, j] = acc

        with tc.tile_pool(name="head", bufs=1) as head:
            w_raw = head.tile([P, 2, G, 4, XD], BF16)
            w_grp = head.tile([P, 2, XD, 4], BF16, align_bytes=64)
            y_raw = head.tile([P, NT, YD], BF16)
            y_grp = head.tile([P, 4, 2 * P * 4], BF16, align_bytes=64)
            pre = head.tile([P, NT, XD], F32)

            nc.vector.memset(params[:], 0.0)
            nc.vector.memset(ones[:], 1.0)
            make_identity(nc, ident16[:])
            make_identity(nc, ident32[:])

            def load_w(which, src, g):
                nc.sync.dma_start(out=w_raw[:, which, g],
                                  in_=src[g * 512:(g + 1) * 512, :].rearrange("(p j) c -> p j c", j=4))

            def load_y(h):
                nc.sync.dma_start(out=y_raw[:, 2 * h:2 * h + 2, :], in_=y_rows[:, 2 * h:2 * h + 2, :])

            load_w(SIG, We_sig, 0)
            load_y(0)
            load_w(SIG, We_sig, 1)
            for h in range(1, 4):
                load_y(h)
            load_w(MU, We_mu, 0)
            load_w(MU, We_mu, 1)
            nc.scalar.dma_start(out=params[ROW_MU:ROW_MU + KC, :], in_=phi_mus)
            nc.scalar.dma_start(out=params[ROW_SIG:ROW_SIG + KC, :], in_=phi_sigs)
            nc.scalar.dma_start(out=params[ROW_BMU:ROW_BMU + 1, :], in_=be_mu.unsqueeze(0))
            nc.scalar.dma_start(out=params[ROW_BSIG:ROW_BSIG + 1, :], in_=be_sig.unsqueeze(0))
            nc.scalar.dma_start(out=params[ROW_LOGIT:ROW_LOGIT + 1, 0:KC], in_=phi_logits.unsqueeze(0))

            def spread_row(out, row, width):
                nc.tensor.matmul(out, lhsT=ident16[:, row:row + 1].to_broadcast([P, P]), rhs=params[:, 0:width],
                                 start=True, stop=True)

            def interleave_w(which, g):
                nc.vector.tensor_copy(out=w_grp[:, g].rearrange("p (c i) t -> p c t i", i=4),
                                      in_=w_raw[:, which, g].rearrange("p t (c i) -> p c t i", i=4))

            def quantize_w(which, g):
                nc.vector.quantize_mx(out=w_codes[:, which, g, :].bitcast(FP8X4), scales=w_scales[:, which, g, :],
                                      in_=w_grp[:, g].rearrange("p c t -> p (c t)"))

            y_words = y_raw[:].bitcast(F32)

            def turn_y(h):
                for g in range(G):
                    slot = (G * h + g) % 4
                    xt = bank(slot, [P, 2, 2, P])
                    for q in range(2):
                        for u in range(2):
                            nc.tensor.transpose(xt[:, q, u, :],
                                                y_words[:, 2 * h + q, 256 * g + u:256 * (g + 1):2], ident32[:])
                    nc.scalar.copy(out=y_grp[:, slot, :].bitcast(F32).rearrange("p (q r u) -> p q r u", q=2, u=2),
                                   in_=xt[:].rearrange("p q u r -> p q r u"))

            def quantize_y(h, g):
                rows = slice(2 * h * P, 2 * (h + 1) * P)
                nc.vector.quantize_mx(out=y_codes[:, g, rows].bitcast(FP8X4), scales=y_scales[:, g, rows],
                                      in_=y_grp[:, (G * h + g) % 4, :])

            def pre_act(t):
                acc = encode_rows(4 + t % 3, SIG, t)
                nc.vector.tensor_tensor(out=pre[:, t, :], in0=acc[:], in1=bias_sig[:], op=ALU.add)

            def exp_neg_abs(h):
                two = slice(2 * h, 2 * h + 2)
                nc.vector.scalar_tensor_tensor(out=soft[:, two, :], in0=pre[:, two, :], scalar=-1.0,
                                               in1=pre[:, two, :], op0=ALU.mult, op1=ALU.min)
                nc.scalar.activation(out=soft[:, two, :], in_=soft[:, two, :], func=ACT.Exp)

            interleave_w(SIG, 0)
            turn_y(0)
            par_ps = bank(7, [P, NJ, P], BF16)
            for j in range(NJ):
                nc.tensor.transpose(par_ps[:, j, :], params[:, j * P:(j + 1) * P], ident16[:])
            nc.scalar.copy(out=par_t[:], in_=par_ps[:, :, 0:ROW_BMU + 1])
            bs_ps = bank(6, [P, XD])
            spread_row(bs_ps[:], ROW_BSIG, XD)
            nc.scalar.copy(out=bias_sig[:], in_=bs_ps[:])
            bm_ps = bank(5, [P, XD])
            spread_row(bm_ps[:], ROW_BMU, XD)
            nc.scalar.copy(out=bias_mu[:], in_=bm_ps[:])

            phi_sig_t = par_t[:, :, ROW_SIG:ROW_SIG + KC]
            nc.vector.reciprocal(out=inv_p[:], in_=phi_sig_t)
            quantize_w(SIG, 0)
            interleave_w(SIG, 1)
            nc.vector.tensor_tensor(out=centre[:], in0=par_t[:, :, ROW_MU:ROW_MU + KC],
                                    in1=par_t[:, :, ROW_BMU:ROW_BMU + 1].to_broadcast([P, NJ, KC]), op=ALU.subtract)
            nc.vector.tensor_tensor(out=inv_p2[:], in0=inv_p[:], in1=inv_p[:], op=ALU.mult)
            turn_y(1)
            quantize_y(0, 0)
            quantize_w(SIG, 1)
            quantize_y(0, 1)
            for h in range(4):
                if h + 1 < 4:
                    quantize_y(h + 1, 0)
                    quantize_y(h + 1, 1)
                pre_act(2 * h)
                pre_act(2 * h + 1)
                if h + 2 < 4:
                    turn_y(h + 2)
                if h >= 2:
                    interleave_w(MU, h - 2)
                exp_neg_abs(h)
            quantize_w(MU, 0)
            quantize_w(MU, 1)

            nc.scalar.activation(out=ln_p[:], in_=phi_sig_t, func=ACT.Ln)
            for h in range(4):
                two = slice(2 * h, 2 * h + 2)
                nc.scalar.activation(out=soft[:, two, :], in_=soft[:, two, :], func=ACT.Ln,
                                     scale=EPS_FACTOR, bias=EPS_FACTOR)
                nc.vector.scalar_tensor_tensor(out=soft[:, two, :], in0=pre[:, two, :], scalar=0.0,
                                               in1=soft[:, two, :], op0=ALU.max, op1=ALU.add)
                nc.sync.dma_start(out=sig_rows[:, two, :], in_=soft[:, two, :])

        for j in range(NJ):
            encode_mu_t(0, j)
        const_ps = bank(7, [P, 2, KC])
        spread_row(const_ps[:, 0, :], ROW_LOGIT, KC)
        for j in range(NJ):
            nc.tensor.matmul(const_ps[:, 1, :], lhsT=ones[:].to_broadcast([P, P]), rhs=ln_p[:, j, :],
                             start=(j == 0), stop=(j == NJ - 1))
        nc.vector.tensor_copy(out=logit[:], in_=const_ps[:, 0, :])
        use = 8
        for c in range(N // CH):
            for j in range(NJ):
                st = bank(4 + use % 3, [P, TPC, P])
                use += 1
                for q in range(TPC):
                    nc.tensor.transpose(st[:, q, :], soft[:, c * TPC + q, j * P:(j + 1) * P], ident32[:])
                nc.scalar.activation(out=ln_s[:, j, c * CH:(c + 1) * CH], in_=st[:].rearrange("p q r -> p (q r)"),
                                     func=ACT.Ln)
        for t in range(NT):
            acc = encode_rows(4 + use % 3, MU, t)
            use += 1
            nc.vector.tensor_tensor(out=mu_out[:, t % 4, :], in0=acc[:], in1=bias_mu[:], op=ALU.add)
            if t == 0:
                nc.vector.tensor_tensor(out=z_const[:], in0=logit[:], in1=const_ps[:, 1, :], op=ALU.subtract)
            if t % 2 == 1:
                nc.sync.dma_start(out=mu_rows[:, t - 1:t + 1, :], in_=mu_out[:, t % 4 - 1:t % 4 + 1, :])

        main = ctx.enter_context(tc.tile_pool(name="main", bufs=1))
        ratio = main.tile([P, SIG_RING, CH], F32)
        prod = main.tile([P, PERIODS, CH], F32)
        z_ln = main.tile([P, NT, KC], F32)
        z_lin = main.tile([P, NT, KC], F32)
        ln_terms = main.tile([P, TPC, P], F32)

        def sigmoid(x):
            i, j = divmod(x, NJ)
            c, k = divmod(i, KC)
            nc.scalar.activation(out=ratio[:, x % SIG_RING, :], in_=ln_s[:, j, c * CH:(c + 1) * CH],
                                 func=ACT.Sigmoid, scale=-1.0, bias=ln_p[:, j, k:k + 1])

        def r_of(i, j):
            return ratio[:, (NJ * i + j) % SIG_RING, :]

        def t_of(i, j):
            return t_ring[:, (NJ * i + j) % T_RING, :]

        def whiten(i, j):
            c, k = divmod(i, KC)
            nc.vector.scalar_tensor_tensor(out=t_of(i, j), in0=mu_t[c, j][:], scalar=centre[:, j, k:k + 1],
                                           in1=r_of(i, j), op0=ALU.subtract, op1=ALU.mult)

        def square_scalar(i, j):
            k = i % KC
            nc.scalar.activation(out=t_of(i, j), in_=t_of(i, j), func=ACT.Square, scale=inv_p[:, j, k:k + 1])

        def square_vector(i, j):
            k = i % KC
            nc.vector.scalar_tensor_tensor(out=t_of(i, j), in0=t_of(i, j), scalar=inv_p2[:, j, k:k + 1],
                                           in1=t_of(i, j), op0=ALU.mult, op1=ALU.mult)

        def pair_products(i):
            base = (NJ * i) % SIG_RING
            nc.gpsimd.tensor_tensor(out=pair[:], in0=ratio[:, base:base + NJ:2, :],
                                    in1=ratio[:, base + 1:base + NJ:2, :], op=ALU.mult)

        def full_product(i):
            nc.vector.tensor_tensor(out=prod[:, i, :], in0=pair[:, 0, :], in1=pair[:, 1, :], op=ALU.mult)

        acc_of = {}

        def turn_squares(i):
            acc = bank(4 + i % 2, [P, TPC, P])
            for q in range(TPC):
                for j in range(NJ):
                    nc.tensor.matmul(acc[:, q, :], lhsT=t_of(i, j)[:, q * P:(q + 1) * P], rhs=ident32[:],
                                     is_transpose=True, start=(j == 0), stop=(j == NJ - 1))
            acc_of[i] = acc

        def reduce_squares(i):
            c, k = divmod(i, KC)
            nc.vector.tensor_reduce(out=z_sq[:, c * TPC:(c + 1) * TPC, k], in_=acc_of[i][:], axis=AX.X, op=ALU.add)

        turned = {}

        def turn_product(i):
            pt = bank(6 + i % 2, [P, TPC, P])
            for q in range(TPC):
                nc.tensor.transpose(pt[:, q, :], prod[:, i, q * P:(q + 1) * P], ident32[:])
            turned[i] = pt

        def log_product(i):
            c, k = divmod(i, KC)
            for q in range(TPC):
                nc.scalar.activation(out=ln_terms[:, q, :], in_=turned[i][:, q, :], func=ACT.Ln,
                                     accum_out=z_ln[:, c * TPC + q, k:k + 1])

        ln_start = PERIODS - LN_LEN
        sigs_of, logs_of = [], []
        sig_next, ln_next = LEAD * NJ, 0
        for i in range(PERIODS + 3):
            sig_goal, ln_goal = sig_next, ln_next
            if i < ln_start:
                sig_goal = LEAD * NJ + -(-NJ * (PERIODS - LEAD) * (i + 1) // ln_start)
            else:
                want = -(-(PERIODS - ln_next) // max(PERIODS + 0 - i, 1))
                ln_goal = min(ln_next + want, i, PERIODS)
            sigs_of.append(list(range(sig_next, sig_goal)))
            logs_of.append(list(range(ln_next, ln_goal)))
            sig_next, ln_next = sig_goal, ln_goal

        for x in range(LEAD * NJ):
            sigmoid(x)
            if x == NJ - 1:
                pair_products(0)
        sq_credit = 0.0
        for i in range(PERIODS + 2):
            sigs, logs = sigs_of[i], logs_of[i]
            on_scalar = 0
            if 1 <= i <= PERIODS:
                table_work = len(sigs) + LOG_COST * len(logs) + (TABLE_SWITCH if i == ln_start else 0)
                sq_credit += min(max(((VECTOR_FIXED if i < PERIODS else 1) + NJ - table_work) / 2, 0), NJ)
                on_scalar = min(int(sq_credit), NJ)
                sq_credit -= on_scalar

            for s in range(max(len(sigs), len(logs), on_scalar)):
                if s < len(sigs):
                    sigmoid(sigs[s])
                if s < len(logs):
                    log_product(logs[s])
                    if s + 2 < len(logs):
                        turn_product(logs[s + 2])
                if s < on_scalar:
                    square_scalar(i - 1, s)

            if 1 <= i <= PERIODS:
                for j in range(on_scalar, NJ):
                    square_vector(i - 1, j)
            if i < PERIODS:
                full_product(i)
                if i + 1 < PERIODS:
                    pair_products(i + 1)
                for j in range(NJ):
                    whiten(i, j)
            if i == PERIODS + 1:
                nc.vector.tensor_tensor(out=z_lin[:], in0=z_ln[:],
                                        in1=z_const[:].unsqueeze(1).to_broadcast([P, NT, KC]), op=ALU.add)
            if i >= 2:
                reduce_squares(i - 2)
            if i == KC - 1:
                for j in range(NJ):
                    encode_mu_t(1, j)
            for x in logs_of[i + 1][:2]:
                turn_product(x)
            if 1 <= i <= PERIODS:
                turn_squares(i - 1)

        z = keep.tile([P, NT, KC], F32)
        top = keep.tile([P, NT], F32)
        e = keep.tile([P, NT, KC], F32)
        total = keep.tile([P, NT], F32)
        nc.vector.scalar_tensor_tensor(out=z[:], in0=z_sq[:], scalar=-0.5, in1=z_lin[:], op0=ALU.mult, op1=ALU.add)
        nc.vector.tensor_reduce(out=top[:], in_=z[:], axis=AX.X, op=ALU.max)
        nc.vector.tensor_tensor(out=z[:], in0=z[:], in1=top[:].unsqueeze(2).to_broadcast([P, NT, KC]),
                                op=ALU.subtract)
        nc.scalar.activation(out=e[:], in_=z[:], func=ACT.Exp)
        nc.vector.tensor_reduce(out=total[:], in_=e[:], axis=AX.X, op=ALU.add)
        nc.scalar.activation(out=total[:], in_=total[:], func=ACT.Ln)
        nc.vector.tensor_tensor(out=e[:], in0=z[:], in1=total[:].unsqueeze(2).to_broadcast([P, NT, KC]),
                                op=ALU.subtract)
        nc.sync.dma_start(out=z_rows, in_=e[:])
